import numpy as np
import ml_dtypes


def mxq(x, axis, fmt="e4m3"):
    dtype, down = {"e4m3": (ml_dtypes.float8_e4m3fn, 7), "e5m2": (ml_dtypes.float8_e5m2, 14)}[fmt]
    v = np.moveaxis(np.asarray(x, np.float32).astype(ml_dtypes.bfloat16).astype(np.float64), axis, -1)
    blocks = v.reshape(v.shape[:-1] + (-1, 32))
    amax = np.abs(blocks).max(-1, keepdims=True)
    byte = np.maximum(np.where(amax > 0, np.frexp(amax)[1] - 1 + 127, 0) - down, 1)
    scale = np.exp2(byte - 127.0)
    codes = (blocks / scale).astype(np.float32).astype(dtype).astype(np.float64)
    return np.moveaxis((codes * scale).reshape(v.shape), -1, axis)


WIDE = False


def mx_kscale(k):
    if not WIDE:
        return np.ones(k)
    levels = np.array([10, -10, 5, -5, 0])
    if k % 512:
        return np.exp2(np.random.permutation(np.resize(levels, k // 32))).repeat(32)
    a = np.empty((k // 512, 16))
    for p in range(k // 512):
        a[p, :8] = np.random.permutation(np.resize(levels, 8))
        for g in range(8):
            far = levels[np.abs(levels - a[p, g]) >= 10]
            a[p, g + 8] = far[np.random.randint(len(far))]
    return np.exp2(a.ravel()).repeat(32)


BF16 = ml_dtypes.bfloat16


def bf(x):
    return np.asarray(x, np.float32).astype(BF16)


def f64(x):
    return np.asarray(x).astype(np.float64)


B, IN, HID, N, NM = 2, 128, 384, 512, 5
C = IN + HID


def setup_inputs():
    s = mx_kscale(N)
    return {"x": bf(np.random.standard_normal((B, C, N)) * s),
            "support0": bf(np.random.standard_normal((N, N)) * 0.7 / np.sqrt(N) * s[:, None] / s[None, :]),
            "support1": bf(np.random.standard_normal((N, N)) * 0.7 / np.sqrt(N) * s[:, None] / s[None, :])}


def reference(x, support0, support1):
    x0 = f64(x)
    xq = mxq(x0, 2, "e4m3")
    a0q = mxq(f64(support0).T, 0, "e4m3")
    a1q = mxq(f64(support1).T, 0, "e4m3")
    x1_0 = xq @ a0q
    x2_0 = 2.0 * (mxq(x1_0, 2, "e4m3") @ a0q) - x0
    x1_1 = xq @ a1q
    x2_1 = 2.0 * (mxq(x1_1, 2, "e4m3") @ a1q) - x0
    return np.concatenate([x1_0, x2_0, x1_1, x2_1], axis=1)

@@ -1,0 +1,233 @@
+from contextlib import ExitStack
+
+import concourse.mybir as mybir
+from concourse.masks import make_identity
+
+F32 = mybir.dt.float32
+BF16 = mybir.dt.bfloat16
+U32 = mybir.dt.uint32
+U8 = mybir.dt.uint8
+FP8X4 = mybir.dt.float8_e4m3fn_x4
+MULT = mybir.AluOpType.mult
+SUBTRACT = mybir.AluOpType.subtract
+
+P = 128
+NODES = 512
+FLOPS = 4 * 2 * 1024 * NODES * NODES
+
+
+def tile_dcgrucell_pa_kernel(tc, x, support0, support1, out):
+    nc = tc.nc
+    with ExitStack() as ctx:
+        keep = ctx.enter_context(tc.tile_pool(name="keep", bufs=1))
+        psum = ctx.enter_context(tc.psum_pool(name="psum", bufs=8))
+        ctx.enter_context(tc.manual_schedule())
+
+        a_sb = [keep.tile([P, 4 * NODES], BF16, name="a_sb%d" % s) for s in range(2)]
+        x_sb = keep.tile([P, 8 * NODES], BF16, name="x_sb")
+        ident = keep.tile([P, P], F32, name="ident")
+        a_grp = [keep.tile([P, 4 * NODES], BF16, name="a_grp%d" % s, align_bytes=64) for s in range(2)]
+        x_grp = keep.tile([P, 4 * 1024], BF16, name="x_grp", align_bytes=64)
+        y_grp = [keep.tile([P, 4 * 1024], BF16, name="y_grp%d" % s, align_bytes=64) for s in range(2)]
+        a_codes = [keep.tile([P, NODES], U32, name="a_codes%d" % s, align_bytes=64) for s in range(2)]
+        a_scales = [keep.tile([P, NODES], U8, name="a_scales%d" % s, align_bytes=64) for s in range(2)]
+        x_codes = keep.tile([P, 1024], U32, name="x_codes", align_bytes=64)
+        x_scales = keep.tile([P, 1024], U8, name="x_scales", align_bytes=64)
+        y_codes = [keep.tile([P, 1024], U32, name="y_codes%d" % s, align_bytes=64) for s in range(2)]
+        y_scales = [keep.tile([P, 1024], U8, name="y_scales%d" % s, align_bytes=64) for s in range(2)]
+        o_sb = [[keep.tile([P, 4 * NODES], F32, name="o_sb%d_%d" % (seg, b)) for b in range(2)] for seg in range(4)]
+
+        for h in range(2):
+            nc.sync.dma_start(
+                out=a_sb[0][:, 1024 * h : 1024 * h + 1024].rearrange("p (t m) -> p t m", t=2),
+                in_=support0.rearrange("(p t) m -> p t m", t=4)[:, 2 * h : 2 * h + 2, :],
+            )
+        for h in range(2):
+            nc.sync.dma_start(
+                out=x_sb[:, 1024 * h : 1024 * h + 1024].rearrange("p (i m) -> p i m", i=2),
+                in_=x[0].rearrange("(p i) m -> p i m", i=4)[:, 2 * h : 2 * h + 2, :],
+            )
+        nc.sync.dma_start(out=x_sb[:, 2048:4096], in_=x[1].rearrange("(p i) m -> p (i m)", i=4))
+        nc.sync.dma_start(out=a_sb[1][:], in_=support1.rearrange("(p t) m -> p (t m)", t=4))
+        make_identity(nc, ident[:])
+
+        def copy_out(engine, dst, src):
+            if engine is nc.vector:
+                nc.vector.tensor_copy(out=dst, in_=src)
+            else:
+                nc.scalar.copy(out=dst, in_=src)
+
+        def transpose_pair(src, row_tiles):
+            words = src[:].bitcast(F32)
+            bank = psum.tile([P, 512], F32, name="bank")
+            for k, rt in enumerate(row_tiles):
+                for w in range(2):
+                    nc.tensor.transpose(
+                        bank[:, 256 * w + P * k : 256 * w + P * k + P],
+                        words[:, 256 * rt + w : 256 * rt + 256 : 2],
+                        ident[:],
+                    )
+            return bank
+
+        def regroup(engine, bank, grp, c0):
+            copy_out(
+                engine,
+                grp[:].bitcast(F32)[:, 2 * c0 : 2 * c0 + 512].rearrange("p (c w) -> p c w", w=2),
+                bank[:].rearrange("p (w c) -> p c w", w=2),
+            )
+
+        def quantise(grp, codes, scales, c0):
+            nc.vector.quantize_mx(
+                out=codes[:, c0 : c0 + 256].bitcast(FP8X4),
+                scales=scales[:, c0 : c0 + 256],
+                in_=grp[:, 4 * c0 : 4 * c0 + 1024],
+            )
+
+        def mx(dst, l_codes, l_scales, l0, r_codes, r_scales, r0, n):
+            nc.tensor.matmul_mx(
+                out=dst,
+                lhsT=l_codes[:, l0 : l0 + P].bitcast(FP8X4),
+                lhsT_scale=l_scales[:, l0 : l0 + P],
+                rhs=r_codes[:, r0 : r0 + n].bitcast(FP8X4),
+                rhs_scale=r_scales[:, r0 : r0 + n],
+                start=True,
+                stop=True,
+            )
+
+        def rows_by_support(l_codes, l_scales, n):
+            s = n // 4
+            banks = []
+            for j in (2 * (n % 4), 2 * (n % 4) + 1):
+                bank = psum.tile([P, 512], F32, name="bank")
+                mx(bank[:], l_codes, l_scales, P * j, a_codes[s], a_scales[s], 0, NODES)
+                banks.append(bank)
+            return banks
+
+        def x1_passes(n):
+            return rows_by_support(x_codes, x_scales, n)
+
+        def x2_passes(n):
+            return rows_by_support(y_codes[n // 4], y_scales[n // 4], n)
+
+        def x1t_passes(n):
+            s = n // 4
+            banks = []
+            for j in (2 * (n % 4), 2 * (n % 4) + 1):
+                bank = psum.tile([P, 512], F32, name="bank")
+                for t in range(4):
+                    mx(bank[:, P * t : P * t + P], a_codes[s], a_scales[s], P * t,
+                       x_codes, x_scales, P * j, P)
+                banks.append(bank)
+            return banks
+
+        def natural(ap):
+            return ap.rearrange("p (q t) -> p q t", t=4)
+
+        def by_remainder(ap):
+            return ap.rearrange("p (t q) -> p q t", t=4)
+
+        def store(seg, m, first, count):
+            b, i0 = m // 2, 2 * (m % 2) + first
+            nc.sync.dma_start(
+                out=out[b, 512 * seg : 512 * seg + 512, :].rearrange("(p i) n -> p i n", i=4)[:, i0 : i0 + count, :],
+                in_=o_sb[seg][b][:, 512 * i0 : 512 * (i0 + count)].rearrange("p (i n) -> p i n", i=count),
+            )
+
+        def x1_out(n, banks, tile_by_tile=False):
+            seg, m = 2 * (n // 4), n % 4
+            for k in range(2):
+                i = 2 * (m % 2) + k
+                nc.scalar.copy(out=natural(o_sb[seg][m // 2][:, 512 * i : 512 * i + 512]), in_=by_remainder(banks[k][:]))
+                if tile_by_tile:
+                    store(seg, m, k, 1)
+            if not tile_by_tile:
+                store(seg, m, 0, 2)
+
+        def x1t_out(engine, n, banks):
+            s, m = n // 4, n % 4
+            for k in range(2):
+                j = 2 * m + k
+                copy_out(
+                    engine,
+                    y_grp[s][:, 512 * j : 512 * j + 512].rearrange("p (r t) -> p r t", t=4),
+                    banks[k][:].rearrange("p (t r) -> p r t", t=4),
+                )
+
+        def quantise_x1t(n):
+            s = n // 4
+            quantise(y_grp[s], y_codes[s], y_scales[s], 256 * (n % 4))
+
+        def x2_out(n, banks, tile_by_tile=False):
+            seg, m = 2 * (n // 4) + 1, n % 4
+            for k in range(2):
+                i = 2 * (m % 2) + k
+                j = 2 * m + k
+                nc.vector.scalar_tensor_tensor(
+                    out=natural(o_sb[seg][m // 2][:, 512 * i : 512 * i + 512]),
+                    in0=by_remainder(banks[k][:]),
+                    scalar=2.0,
+                    in1=natural(x_sb[:, 512 * j : 512 * j + 512]),
+                    op0=MULT,
+                    op1=SUBTRACT,
+                )
+                if tile_by_tile:
+                    store(seg, m, k, 1)
+            if not tile_by_tile:
+                store(seg, m, 0, 2)
+
+        a_banks = [transpose_pair(a_sb[0], [2 * e, 2 * e + 1]) for e in range(2)]
+        x_banks = [transpose_pair(x_sb, [2 * m, 2 * m + 1]) for m in range(4)]
+        regroup(nc.vector, a_banks[0], a_grp[0], 0)
+        regroup(nc.scalar, a_banks[1], a_grp[0], 256)
+        for e in range(2):
+            quantise(a_grp[0], a_codes[0], a_scales[0], 256 * e)
+        for m in range(3):
+            regroup(nc.scalar, x_banks[m], x_grp, 256 * m)
+            quantise(x_grp, x_codes, x_scales, 256 * m)
+
+        t_banks = []
+
+        def vector_copy(step):
+            if step == 0:
+                regroup(nc.vector, x_banks[3], x_grp, 768)
+            elif step < 3:
+                x1t_out(nc.vector, step - 1, t_banks[step - 1])
+            else:
+                regroup(nc.vector, a_banks[step - 3], a_grp[1], 256 * (step - 3))
+
+        def vector_quantise(step):
+            if step == 0:
+                quantise(x_grp, x_codes, x_scales, 768)
+            elif step < 3:
+                quantise_x1t(step - 1)
+            else:
+                quantise(a_grp[1], a_codes[1], a_scales[1], 256 * (step - 3))
+
+        for n in range(4):
+            b1 = x1_passes(n)
+            if n < 2:
+                t_banks.append(x1t_passes(n))
+            if n == 2:
+                a_banks = [transpose_pair(a_sb[1], [2 * e, 2 * e + 1]) for e in range(2)]
+            x1_out(n, b1, tile_by_tile=(n == 0))
+            vector_copy(n)
+            if n > 0:
+                vector_quantise(n - 1)
+        vector_copy(4)
+        vector_quantise(3)
+        vector_quantise(4)
+
+        for k in range(3):
+            for h in range(2):
+                bt = x1t_passes(2 + 2 * k + h)
+                b2 = x2_passes(2 * k + h)
+                x1t_out(nc.scalar, 2 + 2 * k + h, bt)
+                x2_out(2 * k + h, b2)
+                quantise_x1t(2 + 2 * k + h)
+            b1 = x1_passes(4 + k)
+            x1_out(4 + k, b1)
+        b1 = x1_passes(7)
+        b2 = [x2_passes(6), x2_passes(7)]
+        x2_out(6, b2[0])
+        x1_out(7, b1)
+        x2_out(7, b2[1], tile_by_tile=True)

@@ -49,7 +49,14 @@ def tile_dcgrucell_pa_kernel(tc, x, support0, support1, out):
             )
         nc.sync.dma_start(out=x_sb[:, 2048:4096], in_=x[1].rearrange("(p i) m -> p (i m)", i=4))
         nc.sync.dma_start(out=a_sb[1][:], in_=support1.rearrange("(p t) m -> p (t m)", t=4))
+        zeros = keep.tile([P, NODES], BF16, name="zeros")
+        nc.vector.memset(zeros[:], 0.0)
         make_identity(nc, ident[:])
+        idle_bank = psum.tile([P, 512], F32, name="bank")
+
+        def keep_awake(count):
+            for i in range(count):
+                nc.tensor.matmul(out=idle_bank[:], lhsT=zeros[:, 0:P], rhs=zeros[:], start=True, stop=True)
 
         def copy_out(engine, dst, src):
             if engine is nc.vector:
@@ -175,8 +182,14 @@ def tile_dcgrucell_pa_kernel(tc, x, support0, support1, out):
             if not tile_by_tile:
                 store(seg, m, 0, 2)
 
+        keep_awake(3)
         a_banks = [transpose_pair(a_sb[0], [2 * e, 2 * e + 1]) for e in range(2)]
-        x_banks = [transpose_pair(x_sb, [2 * m, 2 * m + 1]) for m in range(4)]
+        keep_awake(2)
+        x_banks = []
+        for m in range(4):
+            x_banks.append(transpose_pair(x_sb, [2 * m, 2 * m + 1]))
+            if m % 2:
+                keep_awake(1)
         regroup(nc.vector, a_banks[0], a_grp[0], 0)
         regroup(nc.scalar, a_banks[1], a_grp[0], 256)
         for e in range(2):

@@ -140,6 +140,16 @@ def tile_dcgrucell_pa_kernel(tc, x, support0, support1, out):
                 in_=o_sb[seg][b][:, 512 * i0 : 512 * (i0 + count)].rearrange("p (i n) -> p i n", i=count),
             )
 
+        def store_pair(seg, m, with_previous, with_next):
+            if with_previous:
+                b = m // 2
+                nc.sync.dma_start(
+                    out=out[b, 512 * seg : 512 * seg + 512, :].rearrange("(p i) n -> p (i n)", i=4),
+                    in_=o_sb[seg][b][:],
+                )
+            elif not with_next:
+                store(seg, m, 0, 2)
+
         def x1_out(n, banks, tile_by_tile=False):
             seg, m = 2 * (n // 4), n % 4
             for k in range(2):
@@ -148,7 +158,7 @@ def tile_dcgrucell_pa_kernel(tc, x, support0, support1, out):
                 if tile_by_tile:
                     store(seg, m, k, 1)
             if not tile_by_tile:
-                store(seg, m, 0, 2)
+                store_pair(seg, m, n in [7], n + 1 in [7])
 
         def x1t_out(engine, n, banks):
             s, m = n // 4, n % 4
@@ -180,7 +190,7 @@ def tile_dcgrucell_pa_kernel(tc, x, support0, support1, out):
                 if tile_by_tile:
                     store(seg, m, k, 1)
             if not tile_by_tile:
-                store(seg, m, 0, 2)
+                store_pair(seg, m, n in [7], n + 1 in [7])
 
         keep_awake(3)
         a_banks = [transpose_pair(a_sb[0], [2 * e, 2 * e + 1]) for e in range(2)]
@@ -243,4 +253,4 @@ def tile_dcgrucell_pa_kernel(tc, x, support0, support1, out):
         b2 = [x2_passes(6), x2_passes(7)]
         x2_out(6, b2[0])
         x1_out(7, b1)
-        x2_out(7, b2[1], tile_by_tile=True)
+        x2_out(7, b2[1])

@@ -174,7 +174,7 @@ def tile_dcgrucell_pa_kernel(tc, x, support0, support1, out):
             s = n // 4
             quantise(y_grp[s], y_codes[s], y_scales[s], 256 * (n % 4))
 
-        def x2_out(n, banks, tile_by_tile=False):
+        def x2_out(n, banks, tile_by_tile=False, stored=True):
             seg, m = 2 * (n // 4) + 1, n % 4
             for k in range(2):
                 i = 2 * (m % 2) + k
@@ -189,7 +189,7 @@ def tile_dcgrucell_pa_kernel(tc, x, support0, support1, out):
                 )
                 if tile_by_tile:
                     store(seg, m, k, 1)
-            if not tile_by_tile:
+            if stored and not tile_by_tile:
                 store_pair(seg, m, n in [7], n + 1 in [7])
 
         keep_awake(3)
@@ -245,10 +245,11 @@ def tile_dcgrucell_pa_kernel(tc, x, support0, support1, out):
                 bt = x1t_passes(2 + 2 * k + h)
                 b2 = x2_passes(2 * k + h)
                 x1t_out(nc.scalar, 2 + 2 * k + h, bt)
-                x2_out(2 * k + h, b2)
+                x2_out(2 * k + h, b2, stored=(h == 0))
                 quantise_x1t(2 + 2 * k + h)
             b1 = x1_passes(4 + k)
             x1_out(4 + k, b1)
+            store(2 * ((2 * k + 1) // 4) + 1, (2 * k + 1) % 4, 0, 2)
         b1 = x1_passes(7)
         b2 = [x2_passes(6), x2_passes(7)]
         x2_out(6, b2[0])

@@ -42,12 +42,13 @@ def tile_dcgrucell_pa_kernel(tc, x, support0, support1, out):
                 out=a_sb[0][:, 1024 * h : 1024 * h + 1024].rearrange("p (t m) -> p t m", t=2),
                 in_=support0.rearrange("(p t) m -> p t m", t=4)[:, 2 * h : 2 * h + 2, :],
             )
-        for h in range(2):
-            nc.sync.dma_start(
-                out=x_sb[:, 1024 * h : 1024 * h + 1024].rearrange("p (i m) -> p i m", i=2),
-                in_=x[0].rearrange("(p i) m -> p i m", i=4)[:, 2 * h : 2 * h + 2, :],
-            )
-        nc.sync.dma_start(out=x_sb[:, 2048:4096], in_=x[1].rearrange("(p i) m -> p (i m)", i=4))
+        for b in range(2):
+            for h in range(2):
+                c0 = 2048 * b + 1024 * h
+                nc.sync.dma_start(
+                    out=x_sb[:, c0 : c0 + 1024].rearrange("p (i m) -> p i m", i=2),
+                    in_=x[b].rearrange("(p i) m -> p i m", i=4)[:, 2 * h : 2 * h + 2, :],
+                )
         nc.sync.dma_start(out=a_sb[1][:], in_=support1.rearrange("(p t) m -> p (t m)", t=4))
         zeros = keep.tile([P, NODES], BF16, name="zeros")
         nc.vector.memset(zeros[:], 0.0)

from contextlib import ExitStack

import concourse.mybir as mybir
from concourse.masks import make_identity

F32 = mybir.dt.float32
BF16 = mybir.dt.bfloat16
U32 = mybir.dt.uint32
U8 = mybir.dt.uint8
FP8X4 = mybir.dt.float8_e4m3fn_x4
MULT = mybir.AluOpType.mult
SUBTRACT = mybir.AluOpType.subtract

P = 128
NODES = 512
FLOPS = 4 * 2 * 1024 * NODES * NODES


def tile_dcgrucell_pa_kernel(tc, x, support0, support1, out):
    nc = tc.nc
    with ExitStack() as ctx:
        keep = ctx.enter_context(tc.tile_pool(name="keep", bufs=1))
        psum = ctx.enter_context(tc.psum_pool(name="psum", bufs=8))
        ctx.enter_context(tc.manual_schedule())

        a_sb = [keep.tile([P, 4 * NODES], BF16, name="a_sb%d" % s) for s in range(2)]
        x_sb = keep.tile([P, 8 * NODES], BF16, name="x_sb")
        ident = keep.tile([P, P], F32, name="ident")
        a_grp = [keep.tile([P, 4 * NODES], BF16, name="a_grp%d" % s, align_bytes=64) for s in range(2)]
        x_grp = keep.tile([P, 4 * 1024], BF16, name="x_grp", align_bytes=64)
        y_grp = [keep.tile([P, 4 * 1024], BF16, name="y_grp%d" % s, align_bytes=64) for s in range(2)]
        a_codes = [keep.tile([P, NODES], U32, name="a_codes%d" % s, align_bytes=64) for s in range(2)]
        a_scales = [keep.tile([P, NODES], U8, name="a_scales%d" % s, align_bytes=64) for s in range(2)]
        x_codes = keep.tile([P, 1024], U32, name="x_codes", align_bytes=64)
        x_scales = keep.tile([P, 1024], U8, name="x_scales", align_bytes=64)
        y_codes = [keep.tile([P, 1024], U32, name="y_codes%d" % s, align_bytes=64) for s in range(2)]
        y_scales = [keep.tile([P, 1024], U8, name="y_scales%d" % s, align_bytes=64) for s in range(2)]
        o_sb = [[keep.tile([P, 4 * NODES], F32, name="o_sb%d_%d" % (seg, b)) for b in range(2)] for seg in range(4)]

        for h in range(2):
            nc.sync.dma_start(
                out=a_sb[0][:, 1024 * h : 1024 * h + 1024].rearrange("p (t m) -> p t m", t=2),
                in_=support0.rearrange("(p t) m -> p t m", t=4)[:, 2 * h : 2 * h + 2, :],
            )
        for b in range(2):
            for h in range(2):
                c0 = 2048 * b + 1024 * h
                nc.sync.dma_start(
                    out=x_sb[:, c0 : c0 + 1024].rearrange("p (i m) -> p i m", i=2),
                    in_=x[b].rearrange("(p i) m -> p i m", i=4)[:, 2 * h : 2 * h + 2, :],
                )
        nc.sync.dma_start(out=a_sb[1][:], in_=support1.rearrange("(p t) m -> p (t m)", t=4))
        zeros = keep.tile([P, NODES], BF16, name="zeros")
        nc.vector.memset(zeros[:], 0.0)
        make_identity(nc, ident[:])
        idle_bank = psum.tile([P, 512], F32, name="bank")

        def keep_awake(count):
            for i in range(count):
                nc.tensor.matmul(out=idle_bank[:], lhsT=zeros[:, 0:P], rhs=zeros[:], start=True, stop=True)

        def copy_out(engine, dst, src):
            if engine is nc.vector:
                nc.vector.tensor_copy(out=dst, in_=src)
            else:
                nc.scalar.copy(out=dst, in_=src)

        def transpose_pair(src, row_tiles):
            words = src[:].bitcast(F32)
            bank = psum.tile([P, 512], F32, name="bank")
            for k, rt in enumerate(row_tiles):
                for w in range(2):
                    nc.tensor.transpose(
                        bank[:, 256 * w + P * k : 256 * w + P * k + P],
                        words[:, 256 * rt + w : 256 * rt + 256 : 2],
                        ident[:],
                    )
            return bank

        def regroup(engine, bank, grp, c0):
            copy_out(
                engine,
                grp[:].bitcast(F32)[:, 2 * c0 : 2 * c0 + 512].rearrange("p (c w) -> p c w", w=2),
                bank[:].rearrange("p (w c) -> p c w", w=2),
            )

        def quantise(grp, codes, scales, c0):
            nc.vector.quantize_mx(
                out=codes[:, c0 : c0 + 256].bitcast(FP8X4),
                scales=scales[:, c0 : c0 + 256],
                in_=grp[:, 4 * c0 : 4 * c0 + 1024],
            )

        def mx(dst, l_codes, l_scales, l0, r_codes, r_scales, r0, n):
            nc.tensor.matmul_mx(
                out=dst,
                lhsT=l_codes[:, l0 : l0 + P].bitcast(FP8X4),
                lhsT_scale=l_scales[:, l0 : l0 + P],
                rhs=r_codes[:, r0 : r0 + n].bitcast(FP8X4),
                rhs_scale=r_scales[:, r0 : r0 + n],
                start=True,
                stop=True,
            )

        def rows_by_support(l_codes, l_scales, n):
            s = n // 4
            banks = []
            for j in (2 * (n % 4), 2 * (n % 4) + 1):
                bank = psum.tile([P, 512], F32, name="bank")
                mx(bank[:], l_codes, l_scales, P * j, a_codes[s], a_scales[s], 0, NODES)
                banks.append(bank)
            return banks

        def x1_passes(n):
            return rows_by_support(x_codes, x_scales, n)

        def x2_passes(n):
            return rows_by_support(y_codes[n // 4], y_scales[n // 4], n)

        def x1t_passes(n):
            s = n // 4
            banks = []
            for j in (2 * (n % 4), 2 * (n % 4) + 1):
                bank = psum.tile([P, 512], F32, name="bank")
                for t in range(4):
                    mx(bank[:, P * t : P * t + P], a_codes[s], a_scales[s], P * t,
                       x_codes, x_scales, P * j, P)
                banks.append(bank)
            return banks

        def natural(ap):
            return ap.rearrange("p (q t) -> p q t", t=4)

        def by_remainder(ap):
            return ap.rearrange("p (t q) -> p q t", t=4)

        def store(seg, m, first, count):
            b, i0 = m // 2, 2 * (m % 2) + first
            nc.sync.dma_start(
                out=out[b, 512 * seg : 512 * seg + 512, :].rearrange("(p i) n -> p i n", i=4)[:, i0 : i0 + count, :],
                in_=o_sb[seg][b][:, 512 * i0 : 512 * (i0 + count)].rearrange("p (i n) -> p i n", i=count),
            )

        def store_pair(seg, m, with_previous, with_next):
            if with_previous:
                b = m // 2
                nc.sync.dma_start(
                    out=out[b, 512 * seg : 512 * seg + 512, :].rearrange("(p i) n -> p (i n)", i=4),
                    in_=o_sb[seg][b][:],
                )
            elif not with_next:
                store(seg, m, 0, 2)

        def x1_out(n, banks, tile_by_tile=False):
            seg, m = 2 * (n // 4), n % 4
            for k in range(2):
                i = 2 * (m % 2) + k
                nc.scalar.copy(out=natural(o_sb[seg][m // 2][:, 512 * i : 512 * i + 512]), in_=by_remainder(banks[k][:]))
                if tile_by_tile:
                    store(seg, m, k, 1)
            if not tile_by_tile:
                store_pair(seg, m, n in [7], n + 1 in [7])

        def x1t_out(engine, n, banks):
            s, m = n // 4, n % 4
            for k in range(2):
                j = 2 * m + k
                copy_out(
                    engine,
                    y_grp[s][:, 512 * j : 512 * j + 512].rearrange("p (r t) -> p r t", t=4),
                    banks[k][:].rearrange("p (t r) -> p r t", t=4),
                )

        def quantise_x1t(n):
            s = n // 4
            quantise(y_grp[s], y_codes[s], y_scales[s], 256 * (n % 4))

        def x2_out(n, banks, tile_by_tile=False, stored=True):
            seg, m = 2 * (n // 4) + 1, n % 4
            for k in range(2):
                i = 2 * (m % 2) + k
                j = 2 * m + k
                nc.vector.scalar_tensor_tensor(
                    out=natural(o_sb[seg][m // 2][:, 512 * i : 512 * i + 512]),
                    in0=by_remainder(banks[k][:]),
                    scalar=2.0,
                    in1=natural(x_sb[:, 512 * j : 512 * j + 512]),
                    op0=MULT,
                    op1=SUBTRACT,
                )
                if tile_by_tile:
                    store(seg, m, k, 1)
            if stored and not tile_by_tile:
                store_pair(seg, m, n in [7], n + 1 in [7])

        keep_awake(3)
        a_banks = [transpose_pair(a_sb[0], [2 * e, 2 * e + 1]) for e in range(2)]
        keep_awake(2)
        x_banks = []
        for m in range(4):
            x_banks.append(transpose_pair(x_sb, [2 * m, 2 * m + 1]))
            if m % 2:
                keep_awake(1)
        regroup(nc.vector, a_banks[0], a_grp[0], 0)
        regroup(nc.scalar, a_banks[1], a_grp[0], 256)
        for e in range(2):
            quantise(a_grp[0], a_codes[0], a_scales[0], 256 * e)
        for m in range(3):
            regroup(nc.scalar, x_banks[m], x_grp, 256 * m)
            quantise(x_grp, x_codes, x_scales, 256 * m)

        t_banks = []

        def vector_copy(step):
            if step == 0:
                regroup(nc.vector, x_banks[3], x_grp, 768)
            elif step < 3:
                x1t_out(nc.vector, step - 1, t_banks[step - 1])
            else:
                regroup(nc.vector, a_banks[step - 3], a_grp[1], 256 * (step - 3))

        def vector_quantise(step):
            if step == 0:
                quantise(x_grp, x_codes, x_scales, 768)
            elif step < 3:
                quantise_x1t(step - 1)
            else:
                quantise(a_grp[1], a_codes[1], a_scales[1], 256 * (step - 3))

        for n in range(4):
            b1 = x1_passes(n)
            if n < 2:
                t_banks.append(x1t_passes(n))
            if n == 2:
                a_banks = [transpose_pair(a_sb[1], [2 * e, 2 * e + 1]) for e in range(2)]
            x1_out(n, b1, tile_by_tile=(n == 0))
            vector_copy(n)
            if n > 0:
                vector_quantise(n - 1)
        vector_copy(4)
        vector_quantise(3)
        vector_quantise(4)

        for k in range(3):
            for h in range(2):
                bt = x1t_passes(2 + 2 * k + h)
                b2 = x2_passes(2 * k + h)
                x1t_out(nc.scalar, 2 + 2 * k + h, bt)
                x2_out(2 * k + h, b2, stored=(h == 0))
                quantise_x1t(2 + 2 * k + h)
            b1 = x1_passes(4 + k)
            x1_out(4 + k, b1)
            store(2 * ((2 * k + 1) // 4) + 1, (2 * k + 1) % 4, 0, 2)
        b1 = x1_passes(7)
        b2 = [x2_passes(6), x2_passes(7)]
        x2_out(6, b2[0])
        x1_out(7, b1)
        x2_out(7, b2[1])
